import numpy as np
import ml_dtypes


def mxq(x, axis, fmt="e4m3"):
    dtype, down = {"e4m3": (ml_dtypes.float8_e4m3fn, 7), "e5m2": (ml_dtypes.float8_e5m2, 14)}[fmt]
    v = np.moveaxis(np.asarray(x, np.float32).astype(ml_dtypes.bfloat16).astype(np.float64), axis, -1)
    blocks = v.reshape(v.shape[:-1] + (-1, 32))
    amax = np.abs(blocks).max(-1, keepdims=True)
    byte = np.maximum(np.where(amax > 0, np.frexp(amax)[1] - 1 + 127, 0) - down, 1)
    scale = np.exp2(byte - 127.0)
    codes = (blocks / scale).astype(np.float32).astype(dtype).astype(np.float64)
    return np.moveaxis((codes * scale).reshape(v.shape), -1, axis)


WIDE = False


def mx_kscale(k):
    if not WIDE:
        return np.ones(k)
    levels = np.array([10, -10, 5, -5, 0])
    a = np.random.permutation(np.resize(levels, k // 512 * 4)).reshape(k // 512, 4)
    idx = np.arange(k)
    return np.exp2(a[idx // 512, idx % 128 // 32])


BF16 = ml_dtypes.bfloat16


def bf(x):
    return np.asarray(x, np.float32).astype(BF16)


def f64(x):
    return np.asarray(x).astype(np.float64)


B, T, DX, DY, F = 128, 34, 1024, 512, 2
MIN_CONTEXT = 1
G = 1.5 / DY ** 0.25


def setup_inputs():
    s, t = mx_kscale(DX), mx_kscale(DY)
    return {"embeddings": bf(np.random.standard_normal((B, T, DX)) * s),
            "contexts": bf(np.random.standard_normal((B, T, DY)) * G / t),
            "W": bf(np.random.standard_normal((F, DY, DX)) * G / np.sqrt(DX) * t[:, None] / s)}


def reference(embeddings, contexts, W):
    eq = mxq(f64(embeddings)[:, MIN_CONTEXT:T], 2, "e4m3")
    cq = mxq(f64(contexts)[:, MIN_CONTEXT - 1:T - 1], 2, "e4m3")
    wq = mxq(f64(W), 2, "e4m3")
    losses = []
    for step in range(F):
        S = T - step - MIN_CONTEXT
        xw = eq[:, step:] @ wq[step].T
        scores = mxq(xw, 2, "e4m3").transpose(1, 0, 2) @ cq[:, :S].transpose(1, 2, 0)
        pos = np.diagonal(scores, axis1=1, axis2=2)
        m = scores.max(2, keepdims=True)
        lse = np.log(np.exp(scores - m).sum(2)) + m[:, :, 0] - np.log(B * S)
        losses.append((lse - pos).T.reshape(-1))
    return np.concatenate(losses)

@@ -1,0 +1,307 @@
+import math
+from contextlib import ExitStack
+
+import concourse.mybir as mybir
+from concourse.masks import make_identity
+
+FP8X4 = mybir.dt.float8_e4m3fn_x4
+F32 = mybir.dt.float32
+BF16 = mybir.dt.bfloat16
+U32 = mybir.dt.uint32
+U8 = mybir.dt.uint8
+ACT = mybir.ActivationFunctionType
+ALU = mybir.AluOpType
+AX = mybir.AxisListType
+
+P = 128
+B = 128
+DX = 1024
+DY = 512
+F = 2
+NR = 17
+FLOPS = 2 * (33 + 32) * B * DX * DY + 2 * (33 + 32) * B * B * DY
+
+
+def round_times(r):
+    return [1] if r == 0 else [2 * r, 2 * r + 1]
+
+
+def round_pairs(r):
+    return [(0, 0, 0)] if r == 0 else [(0, 0, 0), (1, 0, 1), (2, 1, 0), (3, 1, 1)]
+
+
+def tile_infonceloss_pa_t_kernel(tc, embeddings, contexts, W, out):
+    nc = tc.nc
+    emb2 = embeddings.rearrange("b t d -> b (t d)")
+    ctx2 = contexts.rearrange("b t e -> b (t e)")
+
+    with ExitStack() as ctx:
+        one = ctx.enter_context(tc.tile_pool(name="one", bufs=1))
+        two = ctx.enter_context(tc.tile_pool(name="two", bufs=2))
+        three = ctx.enter_context(tc.tile_pool(name="three", bufs=3))
+        five = ctx.enter_context(tc.tile_pool(name="five", bufs=5))
+        psum = ctx.enter_context(tc.psum_pool(name="psum", bufs=1))
+        ctx.enter_context(tc.manual_schedule())
+
+        xraw, craw, wraw = {}, {}, {}
+
+        def load_x(r):
+            ts = round_times(r)
+            xraw[r] = one.tile([P, len(ts) * DX], BF16, name="xraw%d" % r, tag="xraw%d" % r)
+            nc.sync.dma_start(out=xraw[r][:], in_=emb2[:, ts[0] * DX:(ts[-1] + 1) * DX])
+
+        def load_c(r):
+            n = 2 if r < 16 else 1
+            craw[r] = one.tile([P, n * DY], BF16, name="craw%d" % r, tag="craw%d" % r)
+            nc.sync.dma_start(out=craw[r][:], in_=ctx2[:, 2 * r * DY:(2 * r + n) * DY])
+
+        def load_w(k):
+            wraw[k] = one.tile([P, 4 * DX], BF16, name="wraw%d" % k, tag="wraw%d" % k)
+            src = W[k].rearrange("(u m e) d -> m u (e d)", u=2, e=2)
+            dst = wraw[k][:].rearrange("p (u f) -> p u f", u=2)
+            for u in range(2):
+                nc.sync.dma_start(out=dst[:, u, :], in_=src[:, u, :])
+
+        load_x(0)
+        load_c(0)
+        load_w(0)
+        load_x(1)
+        load_c(1)
+        load_w(1)
+        for r in range(2, NR):
+            load_x(r)
+            load_c(r)
+
+        ident = one.tile([P, P], F32, name="ident", tag="ident")
+        make_identity(nc, ident[:])
+        negmax = one.tile([P, 2, 33], F32, name="negmax", tag="negmax")
+        zsum = one.tile([P, 2, 33], F32, name="zsum", tag="zsum")
+        pos = one.tile([P, 2, 33], F32, name="pos", tag="pos")
+        nc.vector.memset(negmax[:], 0.0)
+        nc.vector.memset(zsum[:], 1.0)
+        nc.vector.memset(pos[:], 0.0)
+        warm = one.tile([P, 1], F32, name="warm", tag="warm")
+        nc.vector.memset(warm[:], 0.0)
+        nc.scalar.activation(out=warm[:], in_=warm[:], func=ACT.Exp)
+
+        wq = {}
+        wsc = {}
+        gw = {}
+        for k in range(F):
+            gw[k] = one.tile([P, 4 * DX], BF16, name="gw%d" % k, tag="gw%d" % k, align_bytes=64)
+            wq[k] = one.tile([P, DX], U32, name="wq%d" % k, tag="wq%d" % k, align_bytes=64)
+            wsc[k] = one.tile([P, DX], U8, name="wsc%d" % k, tag="wsc%d" % k, align_bytes=64)
+
+        def bank(tag):
+            return psum.tile([P, 512], F32, name=tag, tag=tag)
+
+        def copy(eng, o, i):
+            if eng == "v":
+                nc.vector.tensor_copy(out=o, in_=i)
+            else:
+                nc.scalar.copy(out=o, in_=i)
+
+        def transposes(bk, words, nblk):
+            for w in range(nblk):
+                nc.tensor.transpose(bk[:, P * w:P * (w + 1)], words[:, P * w:P * (w + 1)], ident[:])
+
+        def copy_unit(eng, dst, bk, nblk):
+            o = dst.bitcast(F32).rearrange("p (g b u) -> p g b u", g=nblk // 2, u=2)
+            i = bk[:, 0:P * nblk].rearrange("p (g u b) -> p g b u", g=nblk // 2, u=2)
+            copy(eng, o, i)
+
+        def quant(words, scales, grouped):
+            nc.vector.quantize_mx(out=words.bitcast(FP8X4), scales=scales, in_=grouped)
+
+        tb = {}
+        gx, gc, xq, xs, cq, cs = {}, {}, {}, {}, {}, {}
+        xb, gxw, xwq, xws = {}, {}, {}, {}
+        sb, tm = {}, {}
+
+        def st_T(r):
+            ts = round_times(r)
+            xw_ = xraw[r][:].bitcast(F32)
+            for a in range(len(ts)):
+                tb[(r, a)] = bank("TA" if a == 0 else "TB")
+                transposes(tb[(r, a)], xw_[:, 512 * a:512 * (a + 1)], 4)
+            tb[(r, 2)] = bank("TC")
+            transposes(tb[(r, 2)], craw[r][:].bitcast(F32), 4 if r < 16 else 2)
+
+        def st_TW(k, tags):
+            ww = wraw[k][:].bitcast(F32)
+            for tt in range(4):
+                tb[("w", k, tt)] = bank(tags[tt])
+                transposes(tb[("w", k, tt)], ww[:, 512 * tt:512 * (tt + 1)], 4)
+
+        def st_cpW(k, tt, eng):
+            copy_unit(eng, gw[k][:, DX * tt:DX * (tt + 1)], tb[("w", k, tt)], 4)
+
+        def st_QW(k, tt):
+            quant(wq[k][:, 256 * tt:256 * (tt + 1)], wsc[k][:, 256 * tt:256 * (tt + 1)],
+                  gw[k][:, DX * tt:DX * (tt + 1)])
+
+        def st_cpTx(r, a, eng):
+            if a >= len(round_times(r)):
+                return
+            if r not in gx:
+                gx[r] = two.tile([P, 2 * DX], BF16, name="gx", tag="gx", align_bytes=64)
+            copy_unit(eng, gx[r][:, DX * a:DX * (a + 1)], tb[(r, a)], 4)
+
+        def st_cpTc(r, eng):
+            n = 4 if r < 16 else 2
+            gc[r] = two.tile([P, DX], BF16, name="gc", tag="gc", align_bytes=64)
+            copy_unit(eng, gc[r][:, 0:256 * n], tb[(r, 2)], n)
+
+        def st_Qx(r):
+            n = len(round_times(r))
+            xq[r] = three.tile([P, 512], U32, name="xq", tag="xq", align_bytes=64)
+            xs[r] = three.tile([P, 512], U8, name="xs", tag="xs", align_bytes=64)
+            quant(xq[r][:, 0:256 * n], xs[r][:, 0:256 * n], gx[r][:, 0:DX * n])
+
+        def st_Qc(r):
+            n = 2 if r < 16 else 1
+            cq[r] = five.tile([P, 256], U32, name="cq", tag="cq", align_bytes=64)
+            cs[r] = five.tile([P, 256], U8, name="cs", tag="cs", align_bytes=64)
+            quant(cq[r][:, 0:P * n], cs[r][:, 0:P * n], gc[r][:, 0:512 * n])
+
+        def st_MM1(r, q):
+            if q >= len(round_pairs(r)):
+                return
+            k, a = round_pairs(r)[q][1:3]
+            xb[(r, q)] = bank("X%d" % q)
+            for tt in range(4):
+                for g in range(2):
+                    wc = slice((2 * tt + g) * P, (2 * tt + g + 1) * P)
+                    xc = slice((2 * a + g) * P, (2 * a + g + 1) * P)
+                    nc.tensor.matmul_mx(
+                        out=xb[(r, q)][:, P * tt:P * (tt + 1)],
+                        lhsT=wq[k][:, wc].bitcast(FP8X4), lhsT_scale=wsc[k][:, wc],
+                        rhs=xq[r][:, xc].bitcast(FP8X4), rhs_scale=xs[r][:, xc],
+                        start=(g == 0), stop=(g == 1))
+
+        def st_cpX(r, q, eng):
+            if q >= len(round_pairs(r)):
+                return
+            h = q // 2
+            if (r, h) not in gxw:
+                gxw[(r, h)] = two.tile([P, DX], BF16, name="gxw%d" % h, tag="gxw%d" % h, align_bytes=64)
+            o = gxw[(r, h)][:, 512 * (q % 2):512 * (q % 2 + 1)].rearrange("p (b t) -> p b t", t=4)
+            i = xb[(r, q)][:].rearrange("p (t b) -> p b t", t=4)
+            copy(eng, o, i)
+
+        def st_Qxw(r, h):
+            n = len(round_pairs(r)) - 2 * h
+            if n <= 0:
+                return
+            n = min(n, 2)
+            xwq[(r, h)] = three.tile([P, 256], U32, name="xwq%d" % h, tag="xwq%d" % h, align_bytes=64)
+            xws[(r, h)] = three.tile([P, 256], U8, name="xws%d" % h, tag="xws%d" % h, align_bytes=64)
+            quant(xwq[(r, h)][:, 0:P * n], xws[(r, h)][:, 0:P * n], gxw[(r, h)][:, 0:512 * n])
+
+        def st_MM2(r):
+            sb[r] = bank("SC")
+            ts = round_times(r)
+            for q, k, a in round_pairs(r):
+                s = ts[a] - 1 - k
+                lc = slice(P * (q % 2), P * (q % 2 + 1))
+                rc = slice(P * (s % 2), P * (s % 2 + 1))
+                nc.tensor.matmul_mx(
+                    out=sb[r][:, P * q:P * (q + 1)],
+                    lhsT=xwq[(r, q // 2)][:, lc].bitcast(FP8X4), lhsT_scale=xws[(r, q // 2)][:, lc],
+                    rhs=cq[s // 2][:, rc].bitcast(FP8X4), rhs_scale=cs[s // 2][:, rc],
+                    start=True, stop=True)
+
+        def stat_view(t_, r):
+            if r == 0:
+                return t_[:, 0:1, 0:1]
+            return t_[:, :, 2 * r - 1:2 * r + 1]
+
+        def st_SCV(r):
+            nk, na = (1, 1) if r == 0 else (2, 2)
+            nq = nk * na
+            s3 = sb[r][:].rearrange("p (q j) -> p q j", q=4)
+            s4 = sb[r][:].rearrange("p (k a j) -> p k a j", k=2, a=2)[:, 0:nk, 0:na, :]
+            tm[r] = two.tile([P, 4, 32], F32, name="tm", tag="tm")
+            t4 = tm[r][:].rearrange("p (k a) c -> p k a c", k=2)[:, 0:nk, 0:na, :]
+            for qd in range(4):
+                ps = slice(32 * qd, 32 * (qd + 1))
+                nc.vector.tensor_tensor(
+                    out=tm[r][ps, 0:nq, :], in0=s3[ps, 0:nq, ps],
+                    in1=ident[ps, ps].unsqueeze(1).to_broadcast([32, nq, 32]),
+                    op=ALU.mult)
+            nc.vector.tensor_reduce(out=stat_view(negmax, r), in_=s4, axis=AX.X, op=ALU.max, negate=True)
+            nc.vector.tensor_reduce(out=stat_view(pos, r), in_=t4, axis=AX.X, op=ALU.add)
+
+        def st_EXP(r):
+            ts = round_times(r)
+            for q, k, a in round_pairs(r):
+                ix = ts[a] - 1
+                junk = two.tile([P, P], F32, name="junk", tag="junk")
+                nc.scalar.activation(out=junk[:], in_=sb[r][:, P * q:P * (q + 1)], func=ACT.Exp,
+                                     bias=negmax[:, k, ix:ix + 1], scale=1.0,
+                                     accum_out=zsum[:, k, ix:ix + 1])
+
+        def ok(r):
+            return 0 <= r < NR
+
+        for i in range(-1, NR + 2):
+            if ok(i + 1):
+                st_T(i + 1)
+            if i == -1:
+                st_TW(0, ["X0", "X1", "X2", "X3"])
+            if ok(i - 2):
+                st_SCV(i - 2)
+            if ok(i - 1):
+                st_cpX(i - 1, 3, "s")
+            if ok(i + 1):
+                st_cpTx(i + 1, 0, "s")
+                st_cpTx(i + 1, 1, "s")
+                st_cpTc(i + 1, "v")
+                st_Qx(i + 1)
+            if ok(i - 1):
+                st_Qxw(i - 1, 1)
+            if ok(i - 2):
+                st_EXP(i - 2)
+            if ok(i + 1):
+                st_Qc(i + 1)
+            if i == -1:
+                st_cpW(0, 0, "s")
+                st_cpW(0, 1, "v")
+                st_cpW(0, 2, "s")
+                st_QW(0, 0)
+                st_cpW(0, 3, "v")
+                st_QW(0, 1)
+                st_QW(0, 2)
+                st_QW(0, 3)
+            if ok(i):
+                for q in range(4):
+                    st_MM1(i, q)
+            if i == 0:
+                st_TW(1, ["X1", "X2", "X3", "SC"])
+                st_cpW(1, 0, "s")
+                st_cpW(1, 1, "v")
+                st_cpW(1, 2, "s")
+                st_QW(1, 0)
+                st_cpW(1, 3, "v")
+                st_QW(1, 1)
+                st_QW(1, 2)
+                st_QW(1, 3)
+            if ok(i):
+                st_cpX(i, 0, "s")
+                st_cpX(i, 1, "s")
+                st_cpX(i, 2, "v")
+                st_Qxw(i, 0)
+            if ok(i - 1):
+                st_MM2(i - 1)
+
+        rest = one.tile([P, 2, 33], F32, name="rest", tag="rest")
+        lnz = one.tile([P, 2, 33], F32, name="lnz", tag="lnz")
+        loss = one.tile([P, 2, 33], F32, name="loss", tag="loss")
+        for k in range(F):
+            nc.vector.scalar_tensor_tensor(out=rest[:, k, :], in0=negmax[:, k, :],
+                                           scalar=math.log(float(B * (33 - k))), in1=pos[:, k, :],
+                                           op0=ALU.add, op1=ALU.add)
+        nc.scalar.activation(out=lnz[:], in_=zsum[:], func=ACT.Ln)
+        nc.vector.tensor_tensor(out=loss[:], in0=lnz[:], in1=rest[:], op=ALU.subtract)
+        nc.sync.dma_start(out=out[0:B * 33].rearrange("(b s) -> b s", s=33), in_=loss[:, 0, :])
+        nc.sync.dma_start(out=out[B * 33:B * 65].rearrange("(b s) -> b s", s=32), in_=loss[:, 1, 1:33])

@@ -23,11 +23,23 @@ FLOPS = 2 * (33 + 32) * B * DX * DY + 2 * (33 + 32) * B * B * DY
 
 
 def round_times(r):
-    return [1] if r == 0 else [2 * r, 2 * r + 1]
+    return [2 * r + 1, 2 * r + 2] if r < 16 else [33]
 
 
 def round_pairs(r):
-    return [(0, 0, 0)] if r == 0 else [(0, 0, 0), (1, 0, 1), (2, 1, 0), (3, 1, 1)]
+    if r == 0:
+        return [(0, 0, 0), (1, 0, 1), (2, 1, 1)]
+    if r == 16:
+        return [(0, 0, 0), (1, 1, 0)]
+    return [(0, 0, 0), (1, 0, 1), (2, 1, 0), (3, 1, 1)]
+
+
+def round_groups(r):
+    if r == 0:
+        return [(0, 1, 2, 0, 0), (2, 1, 1, 1, 1)]
+    if r == 16:
+        return [(0, 2, 1, 0, 32)]
+    return [(0, 2, 2, 0, 2 * r)]
 
 
 def tile_infonceloss_pa_t_kernel(tc, embeddings, contexts, W, out):
@@ -62,13 +74,11 @@ def tile_infonceloss_pa_t_kernel(tc, embeddings, contexts, W, out):
             for u in range(2):
                 nc.sync.dma_start(out=dst[:, u, :], in_=src[:, u, :])
 
+        load_w(0)
         load_x(0)
         load_c(0)
-        load_w(0)
-        load_x(1)
-        load_c(1)
         load_w(1)
-        for r in range(2, NR):
+        for r in range(1, NR):
             load_x(r)
             load_c(r)
 
@@ -81,8 +91,8 @@ def tile_infonceloss_pa_t_kernel(tc, embeddings, contexts, W, out):
         nc.vector.memset(zsum[:], 1.0)
         nc.vector.memset(pos[:], 0.0)
         warm = one.tile([P, 1], F32, name="warm", tag="warm")
-        nc.vector.memset(warm[:], 0.0)
-        nc.scalar.activation(out=warm[:], in_=warm[:], func=ACT.Exp)
+        nc.vector.memset(warm[:], 1.0)
+        nc.scalar.activation(out=warm[:], in_=warm[:], func=ACT.Ln)
 
         wq = {}
         wsc = {}
@@ -92,7 +102,11 @@ def tile_infonceloss_pa_t_kernel(tc, embeddings, contexts, W, out):
             wq[k] = one.tile([P, DX], U32, name="wq%d" % k, tag="wq%d" % k, align_bytes=64)
             wsc[k] = one.tile([P, DX], U8, name="wsc%d" % k, tag="wsc%d" % k, align_bytes=64)
 
-        def bank(tag):
+        ring_count = [0]
+
+        def ring_bank():
+            tag = "R%d" % (ring_count[0] % 6)
+            ring_count[0] = ring_count[0] + 1
             return psum.tile([P, 512], F32, name=tag, tag=tag)
 
         def copy(eng, o, i):
@@ -118,20 +132,24 @@ def tile_infonceloss_pa_t_kernel(tc, embeddings, contexts, W, out):
         xb, gxw, xwq, xws = {}, {}, {}, {}
         sb, tm = {}, {}
 
-        def st_T(r):
-            ts = round_times(r)
-            xw_ = xraw[r][:].bitcast(F32)
-            for a in range(len(ts)):
-                tb[(r, a)] = bank("TA" if a == 0 else "TB")
-                transposes(tb[(r, a)], xw_[:, 512 * a:512 * (a + 1)], 4)
-            tb[(r, 2)] = bank("TC")
+        def st_Tx(r, a):
+            if a >= len(round_times(r)):
+                return
+            tb[(r, a)] = ring_bank()
+            transposes(tb[(r, a)], xraw[r][:].bitcast(F32)[:, 512 * a:512 * (a + 1)], 4)
+
+        def st_Tc(r):
+            tb[(r, 2)] = ring_bank()
             transposes(tb[(r, 2)], craw[r][:].bitcast(F32), 4 if r < 16 else 2)
 
-        def st_TW(k, tags):
-            ww = wraw[k][:].bitcast(F32)
-            for tt in range(4):
-                tb[("w", k, tt)] = bank(tags[tt])
-                transposes(tb[("w", k, tt)], ww[:, 512 * tt:512 * (tt + 1)], 4)
+        def st_T(r):
+            st_Tx(r, 0)
+            st_Tx(r, 1)
+            st_Tc(r)
+
+        def st_TW(k, tt):
+            tb[("w", k, tt)] = ring_bank()
+            transposes(tb[("w", k, tt)], wraw[k][:].bitcast(F32)[:, 512 * tt:512 * (tt + 1)], 4)
 
         def st_cpW(k, tt, eng):
             copy_unit(eng, gw[k][:, DX * tt:DX * (tt + 1)], tb[("w", k, tt)], 4)
@@ -168,7 +186,7 @@ def tile_infonceloss_pa_t_kernel(tc, embeddings, contexts, W, out):
             if q >= len(round_pairs(r)):
                 return
             k, a = round_pairs(r)[q][1:3]
-            xb[(r, q)] = bank("X%d" % q)
+            xb[(r, q)] = ring_bank()
             for tt in range(4):
                 for g in range(2):
                     wc = slice((2 * tt + g) * P, (2 * tt + g + 1) * P)
@@ -199,7 +217,7 @@ def tile_infonceloss_pa_t_kernel(tc, embeddings, contexts, W, out):
             quant(xwq[(r, h)][:, 0:P * n], xws[(r, h)][:, 0:P * n], gxw[(r, h)][:, 0:512 * n])
 
         def st_MM2(r):
-            sb[r] = bank("SC")
+            sb[r] = psum.tile([P, 512], F32, name="S%d" % (r % 2), tag="S%d" % (r % 2))
             ts = round_times(r)
             for q, k, a in round_pairs(r):
                 s = ts[a] - 1 - k
@@ -211,26 +229,25 @@ def tile_infonceloss_pa_t_kernel(tc, embeddings, contexts, W, out):
                     rhs=cq[s // 2][:, rc].bitcast(FP8X4), rhs_scale=cs[s // 2][:, rc],
                     start=True, stop=True)
 
-        def stat_view(t_, r):
-            if r == 0:
-                return t_[:, 0:1, 0:1]
-            return t_[:, :, 2 * r - 1:2 * r + 1]
-
         def st_SCV(r):
-            nk, na = (1, 1) if r == 0 else (2, 2)
-            nq = nk * na
+            nq = len(round_pairs(r))
             s3 = sb[r][:].rearrange("p (q j) -> p q j", q=4)
-            s4 = sb[r][:].rearrange("p (k a j) -> p k a j", k=2, a=2)[:, 0:nk, 0:na, :]
             tm[r] = two.tile([P, 4, 32], F32, name="tm", tag="tm")
-            t4 = tm[r][:].rearrange("p (k a) c -> p k a c", k=2)[:, 0:nk, 0:na, :]
             for qd in range(4):
                 ps = slice(32 * qd, 32 * (qd + 1))
                 nc.vector.tensor_tensor(
                     out=tm[r][ps, 0:nq, :], in0=s3[ps, 0:nq, ps],
                     in1=ident[ps, ps].unsqueeze(1).to_broadcast([32, nq, 32]),
                     op=ALU.mult)
-            nc.vector.tensor_reduce(out=stat_view(negmax, r), in_=s4, axis=AX.X, op=ALU.max, negate=True)
-            nc.vector.tensor_reduce(out=stat_view(pos, r), in_=t4, axis=AX.X, op=ALU.add)
+            for q0, nk, na, k0, i0 in round_groups(r):
+                v = sb[r][:, P * q0:P * (q0 + nk * na)].rearrange("p (k a j) -> p k a j", k=nk, a=na)
+                nc.vector.tensor_reduce(out=negmax[:, k0:k0 + nk, i0:i0 + na], in_=v,
+                                        axis=AX.X, op=ALU.max, negate=True)
+
+        def st_RED(r):
+            for q0, nk, na, k0, i0 in round_groups(r):
+                v = tm[r][:, q0:q0 + nk * na, :].rearrange("p (k a) c -> p k a c", k=nk)
+                nc.vector.tensor_reduce(out=pos[:, k0:k0 + nk, i0:i0 + na], in_=v, axis=AX.X, op=ALU.add)
 
         def st_EXP(r):
             ts = round_times(r)
@@ -244,55 +261,75 @@ def tile_infonceloss_pa_t_kernel(tc, embeddings, contexts, W, out):
         def ok(r):
             return 0 <= r < NR
 
-        for i in range(-1, NR + 2):
+        for tt in range(4):
+            st_TW(0, tt)
+        st_Tx(0, 0)
+        st_Tx(0, 1)
+        st_cpW(0, 0, "s")
+        st_cpW(0, 1, "v")
+        st_cpW(0, 2, "s")
+        st_QW(0, 0)
+        st_cpW(0, 3, "v")
+        st_QW(0, 1)
+        st_QW(0, 2)
+        st_QW(0, 3)
+        st_Tc(0)
+        st_cpTx(0, 0, "s")
+        st_cpTx(0, 1, "v")
+        for tt in range(4):
+            st_TW(1, tt)
+        st_cpTc(0, "s")
+        st_Qx(0)
+        st_MM1(0, 0)
+        st_MM1(0, 1)
+        st_cpW(1, 0, "s")
+        st_cpW(1, 1, "v")
+        st_cpW(1, 2, "s")
+        st_QW(1, 0)
+        st_cpW(1, 3, "v")
+        st_QW(1, 1)
+        st_QW(1, 2)
+        st_QW(1, 3)
+        st_Qc(0)
+        st_T(1)
+        st_MM1(0, 2)
+        st_cpX(0, 0, "v")
+        st_cpX(0, 1, "s")
+        st_cpTx(1, 0, "s")
+        st_cpTx(1, 1, "v")
+        st_cpTc(1, "s")
+        st_Qx(1)
+        st_cpX(0, 2, "s")
+        st_Qc(1)
+
+        for i in range(1, NR + 2):
             if ok(i + 1):
                 st_T(i + 1)
-            if i == -1:
-                st_TW(0, ["X0", "X1", "X2", "X3"])
+            if ok(i - 1):
+                st_cpX(i - 1, 3, "v")
+                st_Qxw(i - 1, 0)
+                st_Qxw(i - 1, 1)
             if ok(i - 2):
                 st_SCV(i - 2)
-            if ok(i - 1):
-                st_cpX(i - 1, 3, "s")
+                st_RED(i - 2)
             if ok(i + 1):
                 st_cpTx(i + 1, 0, "s")
                 st_cpTx(i + 1, 1, "s")
-                st_cpTc(i + 1, "v")
+                st_cpTc(i + 1, "s")
                 st_Qx(i + 1)
-            if ok(i - 1):
-                st_Qxw(i - 1, 1)
-            if ok(i - 2):
-                st_EXP(i - 2)
-            if ok(i + 1):
-                st_Qc(i + 1)
-            if i == -1:
-                st_cpW(0, 0, "s")
-                st_cpW(0, 1, "v")
-                st_cpW(0, 2, "s")
-                st_QW(0, 0)
-                st_cpW(0, 3, "v")
-                st_QW(0, 1)
-                st_QW(0, 2)
-                st_QW(0, 3)
             if ok(i):
                 for q in range(4):
                     st_MM1(i, q)
-            if i == 0:
-                st_TW(1, ["X1", "X2", "X3", "SC"])
-                st_cpW(1, 0, "s")
-                st_cpW(1, 1, "v")
-                st_cpW(1, 2, "s")
-                st_QW(1, 0)
-                st_cpW(1, 3, "v")
-                st_QW(1, 1)
-                st_QW(1, 2)
-                st_QW(1, 3)
+                st_cpX(i, 0, "v")
+            if ok(i + 1):
+                st_Qc(i + 1)
             if ok(i):
-                st_cpX(i, 0, "s")
                 st_cpX(i, 1, "s")
-                st_cpX(i, 2, "v")
-                st_Qxw(i, 0)
+                st_cpX(i, 2, "s")
             if ok(i - 1):
                 st_MM2(i - 1)
+            if ok(i - 2):
+                st_EXP(i - 2)
 
         rest = one.tile([P, 2, 33], F32, name="rest", tag="rest")
         lnz = one.tile([P, 2, 33], F32, name="lnz", tag="lnz")

@@ -320,7 +320,7 @@ def tile_infonceloss_pa_t_kernel(tc, embeddings, contexts, W, out):
             if ok(i):
                 for q in range(4):
                     st_MM1(i, q)
-                st_cpX(i, 0, "v")
+                st_cpX(i, 0, "s")
             if ok(i + 1):
                 st_Qc(i + 1)
             if ok(i):

@@ -130,7 +130,7 @@ def tile_infonceloss_pa_t_kernel(tc, embeddings, contexts, W, out):
         tb = {}
         gx, gc, xq, xs, cq, cs = {}, {}, {}, {}, {}, {}
         xb, gxw, xwq, xws = {}, {}, {}, {}
-        sb, tm = {}, {}
+        sb = {}
 
         def st_Tx(r, a):
             if a >= len(round_times(r)):
@@ -230,24 +230,17 @@ def tile_infonceloss_pa_t_kernel(tc, embeddings, contexts, W, out):
                     start=True, stop=True)
 
         def st_SCV(r):
-            nq = len(round_pairs(r))
-            s3 = sb[r][:].rearrange("p (q j) -> p q j", q=4)
-            tm[r] = two.tile([P, 4, 32], F32, name="tm", tag="tm")
-            for qd in range(4):
-                ps = slice(32 * qd, 32 * (qd + 1))
-                nc.vector.tensor_tensor(
-                    out=tm[r][ps, 0:nq, :], in0=s3[ps, 0:nq, ps],
-                    in1=ident[ps, ps].unsqueeze(1).to_broadcast([32, nq, 32]),
-                    op=ALU.mult)
+            ts = round_times(r)
+            for q, k, a in round_pairs(r):
+                ix = ts[a] - 1
+                masked = two.tile([P, P], F32, name="masked", tag="masked")
+                nc.vector.scalar_tensor_tensor(
+                    out=masked[:], in0=sb[r][:, P * q:P * (q + 1)], scalar=1.0, in1=ident[:],
+                    op0=ALU.mult, op1=ALU.mult, accum_out=pos[:, k, ix:ix + 1])
             for q0, nk, na, k0, i0 in round_groups(r):
                 v = sb[r][:, P * q0:P * (q0 + nk * na)].rearrange("p (k a j) -> p k a j", k=nk, a=na)
                 nc.vector.tensor_reduce(out=negmax[:, k0:k0 + nk, i0:i0 + na], in_=v,
                                         axis=AX.X, op=ALU.max, negate=True)
-
-        def st_RED(r):
-            for q0, nk, na, k0, i0 in round_groups(r):
-                v = tm[r][:, q0:q0 + nk * na, :].rearrange("p (k a) c -> p k a c", k=nk)
-                nc.vector.tensor_reduce(out=pos[:, k0:k0 + nk, i0:i0 + na], in_=v, axis=AX.X, op=ALU.add)
 
         def st_EXP(r):
             ts = round_times(r)
@@ -311,7 +304,6 @@ def tile_infonceloss_pa_t_kernel(tc, embeddings, contexts, W, out):
                 st_Qxw(i - 1, 1)
             if ok(i - 2):
                 st_SCV(i - 2)
-                st_RED(i - 2)
             if ok(i + 1):
                 st_cpTx(i + 1, 0, "s")
                 st_cpTx(i + 1, 1, "s")

@@ -91,8 +91,8 @@ def tile_infonceloss_pa_t_kernel(tc, embeddings, contexts, W, out):
         nc.vector.memset(zsum[:], 1.0)
         nc.vector.memset(pos[:], 0.0)
         warm = one.tile([P, 1], F32, name="warm", tag="warm")
-        nc.vector.memset(warm[:], 1.0)
-        nc.scalar.activation(out=warm[:], in_=warm[:], func=ACT.Ln)
+        nc.vector.memset(warm[:], 0.0)
+        nc.scalar.activation(out=warm[:], in_=warm[:], func=ACT.Exp)
 
         wq = {}
         wsc = {}
@@ -312,7 +312,7 @@ def tile_infonceloss_pa_t_kernel(tc, embeddings, contexts, W, out):
             if ok(i):
                 for q in range(4):
                     st_MM1(i, q)
-                st_cpX(i, 0, "s")
+                st_cpX(i, 0, "v" if i % 2 == 1 else "s")
             if ok(i + 1):
                 st_Qc(i + 1)
             if ok(i):

@@ -55,6 +55,13 @@ def tile_infonceloss_pa_t_kernel(tc, embeddings, contexts, W, out):
         psum = ctx.enter_context(tc.psum_pool(name="psum", bufs=1))
         ctx.enter_context(tc.manual_schedule())
 
+        zeros = one.tile([P, 512], BF16, name="zeros", tag="zeros")
+        nc.vector.memset(zeros[:], 0.0)
+        dbank = psum.tile([P, 512], F32, name="S1", tag="S1")
+
+        def dummy():
+            nc.tensor.matmul(out=dbank[:], lhsT=zeros[:, 0:P], rhs=zeros[:], start=True, stop=True)
+
         xraw, craw, wraw = {}, {}, {}
 
         def load_x(r):
@@ -254,10 +261,17 @@ def tile_infonceloss_pa_t_kernel(tc, embeddings, contexts, W, out):
         def ok(r):
             return 0 <= r < NR
 
-        for tt in range(4):
-            st_TW(0, tt)
+        for n in range(5):
+            dummy()
+        st_TW(0, 0)
+        st_TW(0, 1)
+        dummy()
+        st_TW(0, 2)
+        st_TW(0, 3)
+        dummy()
         st_Tx(0, 0)
         st_Tx(0, 1)
+        dummy()
         st_cpW(0, 0, "s")
         st_cpW(0, 1, "v")
         st_cpW(0, 2, "s")
@@ -269,8 +283,12 @@ def tile_infonceloss_pa_t_kernel(tc, embeddings, contexts, W, out):
         st_Tc(0)
         st_cpTx(0, 0, "s")
         st_cpTx(0, 1, "v")
-        for tt in range(4):
-            st_TW(1, tt)
+        st_TW(1, 0)
+        dummy()
+        st_TW(1, 1)
+        st_TW(1, 2)
+        dummy()
+        st_TW(1, 3)
         st_cpTc(0, "s")
         st_Qx(0)
         st_MM1(0, 0)

import math
from contextlib import ExitStack

import concourse.mybir as mybir
from concourse.masks import make_identity

FP8X4 = mybir.dt.float8_e4m3fn_x4
F32 = mybir.dt.float32
BF16 = mybir.dt.bfloat16
U32 = mybir.dt.uint32
U8 = mybir.dt.uint8
ACT = mybir.ActivationFunctionType
ALU = mybir.AluOpType
AX = mybir.AxisListType

P = 128
B = 128
DX = 1024
DY = 512
F = 2
NR = 17
FLOPS = 2 * (33 + 32) * B * DX * DY + 2 * (33 + 32) * B * B * DY


def round_times(r):
    return [2 * r + 1, 2 * r + 2] if r < 16 else [33]


def round_pairs(r):
    if r == 0:
        return [(0, 0, 0), (1, 0, 1), (2, 1, 1)]
    if r == 16:
        return [(0, 0, 0), (1, 1, 0)]
    return [(0, 0, 0), (1, 0, 1), (2, 1, 0), (3, 1, 1)]


def round_groups(r):
    if r == 0:
        return [(0, 1, 2, 0, 0), (2, 1, 1, 1, 1)]
    if r == 16:
        return [(0, 2, 1, 0, 32)]
    return [(0, 2, 2, 0, 2 * r)]


def tile_infonceloss_pa_t_kernel(tc, embeddings, contexts, W, out):
    nc = tc.nc
    emb2 = embeddings.rearrange("b t d -> b (t d)")
    ctx2 = contexts.rearrange("b t e -> b (t e)")

    with ExitStack() as ctx:
        one = ctx.enter_context(tc.tile_pool(name="one", bufs=1))
        two = ctx.enter_context(tc.tile_pool(name="two", bufs=2))
        three = ctx.enter_context(tc.tile_pool(name="three", bufs=3))
        five = ctx.enter_context(tc.tile_pool(name="five", bufs=5))
        psum = ctx.enter_context(tc.psum_pool(name="psum", bufs=1))
        ctx.enter_context(tc.manual_schedule())

        zeros = one.tile([P, 512], BF16, name="zeros", tag="zeros")
        nc.vector.memset(zeros[:], 0.0)
        dbank = psum.tile([P, 512], F32, name="S1", tag="S1")

        def dummy():
            nc.tensor.matmul(out=dbank[:], lhsT=zeros[:, 0:P], rhs=zeros[:], start=True, stop=True)

        xraw, craw, wraw = {}, {}, {}

        def load_x(r):
            ts = round_times(r)
            xraw[r] = one.tile([P, len(ts) * DX], BF16, name="xraw%d" % r, tag="xraw%d" % r)
            nc.sync.dma_start(out=xraw[r][:], in_=emb2[:, ts[0] * DX:(ts[-1] + 1) * DX])

        def load_c(r):
            n = 2 if r < 16 else 1
            craw[r] = one.tile([P, n * DY], BF16, name="craw%d" % r, tag="craw%d" % r)
            nc.sync.dma_start(out=craw[r][:], in_=ctx2[:, 2 * r * DY:(2 * r + n) * DY])

        def load_w(k):
            wraw[k] = one.tile([P, 4 * DX], BF16, name="wraw%d" % k, tag="wraw%d" % k)
            src = W[k].rearrange("(u m e) d -> m u (e d)", u=2, e=2)
            dst = wraw[k][:].rearrange("p (u f) -> p u f", u=2)
            for u in range(2):
                nc.sync.dma_start(out=dst[:, u, :], in_=src[:, u, :])

        load_w(0)
        load_x(0)
        load_c(0)
        load_w(1)
        for r in range(1, NR):
            load_x(r)
            load_c(r)

        ident = one.tile([P, P], F32, name="ident", tag="ident")
        make_identity(nc, ident[:])
        negmax = one.tile([P, 2, 33], F32, name="negmax", tag="negmax")
        zsum = one.tile([P, 2, 33], F32, name="zsum", tag="zsum")
        pos = one.tile([P, 2, 33], F32, name="pos", tag="pos")
        nc.vector.memset(negmax[:], 0.0)
        nc.vector.memset(zsum[:], 1.0)
        nc.vector.memset(pos[:], 0.0)
        warm = one.tile([P, 1], F32, name="warm", tag="warm")
        nc.vector.memset(warm[:], 0.0)
        nc.scalar.activation(out=warm[:], in_=warm[:], func=ACT.Exp)

        wq = {}
        wsc = {}
        gw = {}
        for k in range(F):
            gw[k] = one.tile([P, 4 * DX], BF16, name="gw%d" % k, tag="gw%d" % k, align_bytes=64)
            wq[k] = one.tile([P, DX], U32, name="wq%d" % k, tag="wq%d" % k, align_bytes=64)
            wsc[k] = one.tile([P, DX], U8, name="wsc%d" % k, tag="wsc%d" % k, align_bytes=64)

        ring_count = [0]

        def ring_bank():
            tag = "R%d" % (ring_count[0] % 6)
            ring_count[0] = ring_count[0] + 1
            return psum.tile([P, 512], F32, name=tag, tag=tag)

        def copy(eng, o, i):
            if eng == "v":
                nc.vector.tensor_copy(out=o, in_=i)
            else:
                nc.scalar.copy(out=o, in_=i)

        def transposes(bk, words, nblk):
            for w in range(nblk):
                nc.tensor.transpose(bk[:, P * w:P * (w + 1)], words[:, P * w:P * (w + 1)], ident[:])

        def copy_unit(eng, dst, bk, nblk):
            o = dst.bitcast(F32).rearrange("p (g b u) -> p g b u", g=nblk // 2, u=2)
            i = bk[:, 0:P * nblk].rearrange("p (g u b) -> p g b u", g=nblk // 2, u=2)
            copy(eng, o, i)

        def quant(words, scales, grouped):
            nc.vector.quantize_mx(out=words.bitcast(FP8X4), scales=scales, in_=grouped)

        tb = {}
        gx, gc, xq, xs, cq, cs = {}, {}, {}, {}, {}, {}
        xb, gxw, xwq, xws = {}, {}, {}, {}
        sb = {}

        def st_Tx(r, a):
            if a >= len(round_times(r)):
                return
            tb[(r, a)] = ring_bank()
            transposes(tb[(r, a)], xraw[r][:].bitcast(F32)[:, 512 * a:512 * (a + 1)], 4)

        def st_Tc(r):
            tb[(r, 2)] = ring_bank()
            transposes(tb[(r, 2)], craw[r][:].bitcast(F32), 4 if r < 16 else 2)

        def st_T(r):
            st_Tx(r, 0)
            st_Tx(r, 1)
            st_Tc(r)

        def st_TW(k, tt):
            tb[("w", k, tt)] = ring_bank()
            transposes(tb[("w", k, tt)], wraw[k][:].bitcast(F32)[:, 512 * tt:512 * (tt + 1)], 4)

        def st_cpW(k, tt, eng):
            copy_unit(eng, gw[k][:, DX * tt:DX * (tt + 1)], tb[("w", k, tt)], 4)

        def st_QW(k, tt):
            quant(wq[k][:, 256 * tt:256 * (tt + 1)], wsc[k][:, 256 * tt:256 * (tt + 1)],
                  gw[k][:, DX * tt:DX * (tt + 1)])

        def st_cpTx(r, a, eng):
            if a >= len(round_times(r)):
                return
            if r not in gx:
                gx[r] = two.tile([P, 2 * DX], BF16, name="gx", tag="gx", align_bytes=64)
            copy_unit(eng, gx[r][:, DX * a:DX * (a + 1)], tb[(r, a)], 4)

        def st_cpTc(r, eng):
            n = 4 if r < 16 else 2
            gc[r] = two.tile([P, DX], BF16, name="gc", tag="gc", align_bytes=64)
            copy_unit(eng, gc[r][:, 0:256 * n], tb[(r, 2)], n)

        def st_Qx(r):
            n = len(round_times(r))
            xq[r] = three.tile([P, 512], U32, name="xq", tag="xq", align_bytes=64)
            xs[r] = three.tile([P, 512], U8, name="xs", tag="xs", align_bytes=64)
            quant(xq[r][:, 0:256 * n], xs[r][:, 0:256 * n], gx[r][:, 0:DX * n])

        def st_Qc(r):
            n = 2 if r < 16 else 1
            cq[r] = five.tile([P, 256], U32, name="cq", tag="cq", align_bytes=64)
            cs[r] = five.tile([P, 256], U8, name="cs", tag="cs", align_bytes=64)
            quant(cq[r][:, 0:P * n], cs[r][:, 0:P * n], gc[r][:, 0:512 * n])

        def st_MM1(r, q):
            if q >= len(round_pairs(r)):
                return
            k, a = round_pairs(r)[q][1:3]
            xb[(r, q)] = ring_bank()
            for tt in range(4):
                for g in range(2):
                    wc = slice((2 * tt + g) * P, (2 * tt + g + 1) * P)
                    xc = slice((2 * a + g) * P, (2 * a + g + 1) * P)
                    nc.tensor.matmul_mx(
                        out=xb[(r, q)][:, P * tt:P * (tt + 1)],
                        lhsT=wq[k][:, wc].bitcast(FP8X4), lhsT_scale=wsc[k][:, wc],
                        rhs=xq[r][:, xc].bitcast(FP8X4), rhs_scale=xs[r][:, xc],
                        start=(g == 0), stop=(g == 1))

        def st_cpX(r, q, eng):
            if q >= len(round_pairs(r)):
                return
            h = q // 2
            if (r, h) not in gxw:
                gxw[(r, h)] = two.tile([P, DX], BF16, name="gxw%d" % h, tag="gxw%d" % h, align_bytes=64)
            o = gxw[(r, h)][:, 512 * (q % 2):512 * (q % 2 + 1)].rearrange("p (b t) -> p b t", t=4)
            i = xb[(r, q)][:].rearrange("p (t b) -> p b t", t=4)
            copy(eng, o, i)

        def st_Qxw(r, h):
            n = len(round_pairs(r)) - 2 * h
            if n <= 0:
                return
            n = min(n, 2)
            xwq[(r, h)] = three.tile([P, 256], U32, name="xwq%d" % h, tag="xwq%d" % h, align_bytes=64)
            xws[(r, h)] = three.tile([P, 256], U8, name="xws%d" % h, tag="xws%d" % h, align_bytes=64)
            quant(xwq[(r, h)][:, 0:P * n], xws[(r, h)][:, 0:P * n], gxw[(r, h)][:, 0:512 * n])

        def st_MM2(r):
            sb[r] = psum.tile([P, 512], F32, name="S%d" % (r % 2), tag="S%d" % (r % 2))
            ts = round_times(r)
            for q, k, a in round_pairs(r):
                s = ts[a] - 1 - k
                lc = slice(P * (q % 2), P * (q % 2 + 1))
                rc = slice(P * (s % 2), P * (s % 2 + 1))
                nc.tensor.matmul_mx(
                    out=sb[r][:, P * q:P * (q + 1)],
                    lhsT=xwq[(r, q // 2)][:, lc].bitcast(FP8X4), lhsT_scale=xws[(r, q // 2)][:, lc],
                    rhs=cq[s // 2][:, rc].bitcast(FP8X4), rhs_scale=cs[s // 2][:, rc],
                    start=True, stop=True)

        def st_SCV(r):
            ts = round_times(r)
            for q, k, a in round_pairs(r):
                ix = ts[a] - 1
                masked = two.tile([P, P], F32, name="masked", tag="masked")
                nc.vector.scalar_tensor_tensor(
                    out=masked[:], in0=sb[r][:, P * q:P * (q + 1)], scalar=1.0, in1=ident[:],
                    op0=ALU.mult, op1=ALU.mult, accum_out=pos[:, k, ix:ix + 1])
            for q0, nk, na, k0, i0 in round_groups(r):
                v = sb[r][:, P * q0:P * (q0 + nk * na)].rearrange("p (k a j) -> p k a j", k=nk, a=na)
                nc.vector.tensor_reduce(out=negmax[:, k0:k0 + nk, i0:i0 + na], in_=v,
                                        axis=AX.X, op=ALU.max, negate=True)

        def st_EXP(r):
            ts = round_times(r)
            for q, k, a in round_pairs(r):
                ix = ts[a] - 1
                junk = two.tile([P, P], F32, name="junk", tag="junk")
                nc.scalar.activation(out=junk[:], in_=sb[r][:, P * q:P * (q + 1)], func=ACT.Exp,
                                     bias=negmax[:, k, ix:ix + 1], scale=1.0,
                                     accum_out=zsum[:, k, ix:ix + 1])

        def ok(r):
            return 0 <= r < NR

        for n in range(5):
            dummy()
        st_TW(0, 0)
        st_TW(0, 1)
        dummy()
        st_TW(0, 2)
        st_TW(0, 3)
        dummy()
        st_Tx(0, 0)
        st_Tx(0, 1)
        dummy()
        st_cpW(0, 0, "s")
        st_cpW(0, 1, "v")
        st_cpW(0, 2, "s")
        st_QW(0, 0)
        st_cpW(0, 3, "v")
        st_QW(0, 1)
        st_QW(0, 2)
        st_QW(0, 3)
        st_Tc(0)
        st_cpTx(0, 0, "s")
        st_cpTx(0, 1, "v")
        st_TW(1, 0)
        dummy()
        st_TW(1, 1)
        st_TW(1, 2)
        dummy()
        st_TW(1, 3)
        st_cpTc(0, "s")
        st_Qx(0)
        st_MM1(0, 0)
        st_MM1(0, 1)
        st_cpW(1, 0, "s")
        st_cpW(1, 1, "v")
        st_cpW(1, 2, "s")
        st_QW(1, 0)
        st_cpW(1, 3, "v")
        st_QW(1, 1)
        st_QW(1, 2)
        st_QW(1, 3)
        st_Qc(0)
        st_T(1)
        st_MM1(0, 2)
        st_cpX(0, 0, "v")
        st_cpX(0, 1, "s")
        st_cpTx(1, 0, "s")
        st_cpTx(1, 1, "v")
        st_cpTc(1, "s")
        st_Qx(1)
        st_cpX(0, 2, "s")
        st_Qc(1)

        for i in range(1, NR + 2):
            if ok(i + 1):
                st_T(i + 1)
            if ok(i - 1):
                st_cpX(i - 1, 3, "v")
                st_Qxw(i - 1, 0)
                st_Qxw(i - 1, 1)
            if ok(i - 2):
                st_SCV(i - 2)
            if ok(i + 1):
                st_cpTx(i + 1, 0, "s")
                st_cpTx(i + 1, 1, "s")
                st_cpTc(i + 1, "s")
                st_Qx(i + 1)
            if ok(i):
                for q in range(4):
                    st_MM1(i, q)
                st_cpX(i, 0, "v" if i % 2 == 1 else "s")
            if ok(i + 1):
                st_Qc(i + 1)
            if ok(i):
                st_cpX(i, 1, "s")
                st_cpX(i, 2, "s")
            if ok(i - 1):
                st_MM2(i - 1)
            if ok(i - 2):
                st_EXP(i - 2)

        rest = one.tile([P, 2, 33], F32, name="rest", tag="rest")
        lnz = one.tile([P, 2, 33], F32, name="lnz", tag="lnz")
        loss = one.tile([P, 2, 33], F32, name="loss", tag="loss")
        for k in range(F):
            nc.vector.scalar_tensor_tensor(out=rest[:, k, :], in0=negmax[:, k, :],
                                           scalar=math.log(float(B * (33 - k))), in1=pos[:, k, :],
                                           op0=ALU.add, op1=ALU.add)
        nc.scalar.activation(out=lnz[:], in_=zsum[:], func=ACT.Ln)
        nc.vector.tensor_tensor(out=loss[:], in0=lnz[:], in1=rest[:], op=ALU.subtract)
        nc.sync.dma_start(out=out[0:B * 33].rearrange("(b s) -> b s", s=33), in_=loss[:, 0, :])
        nc.sync.dma_start(out=out[B * 33:B * 65].rearrange("(b s) -> b s", s=32), in_=loss[:, 1, 1:33])
